import numpy as np
import ml_dtypes


def mxq(x, axis, fmt="e4m3"):
    dtype, down = {"e4m3": (ml_dtypes.float8_e4m3fn, 7), "e5m2": (ml_dtypes.float8_e5m2, 14)}[fmt]
    v = np.moveaxis(np.asarray(x, np.float32).astype(ml_dtypes.bfloat16).astype(np.float64), axis, -1)
    blocks = v.reshape(v.shape[:-1] + (-1, 32))
    amax = np.abs(blocks).max(-1, keepdims=True)
    byte = np.maximum(np.where(amax > 0, np.frexp(amax)[1] - 1 + 127, 0) - down, 1)
    scale = np.exp2(byte - 127.0)
    codes = (blocks / scale).astype(np.float32).astype(dtype).astype(np.float64)
    return np.moveaxis((codes * scale).reshape(v.shape), -1, axis)


WIDE = False


def mx_kscale(k):
    if not WIDE:
        return np.ones(k)
    levels = np.array([10, -10, 5, -5, 0])
    a = np.random.permutation(np.resize(levels, k // 512 * 4)).reshape(k // 512, 4)
    idx = np.arange(k)
    return np.exp2(a[idx // 512, idx % 128 // 32])


BF16 = ml_dtypes.bfloat16


def bf(x):
    return np.asarray(x, np.float32).astype(BF16)


def f64(x):
    return np.asarray(x).astype(np.float64)


E2M1 = np.array([0.0, 0.5, 1.0, 1.5, 2.0, 3.0, 4.0, 6.0, -0.0, -0.5, -1.0, -1.5, -2.0, -3.0, -4.0, -6.0])


def pack_weight(w, fmt):
    k, n = w.shape
    w = f64(bf(w)).reshape(k // 32, 32, n)
    amax = np.abs(w).max(1)
    if fmt == "e4m3":
        byte = np.frexp(amax)[1] - 1 + 127 - 7
    else:
        mant, ex = np.frexp(amax / 6.0)
        byte = np.where(mant > 0.5, ex, ex - 1) + 127
    byte = np.clip(np.where(amax > 0, byte, 1), 1, 254)
    scaled = (w * np.exp2(127.0 - byte)[:, None, :]).reshape(k, n).astype(np.float32)
    by_word = np.ascontiguousarray(scaled.reshape(k // 512, 128, 4, n).transpose(0, 1, 3, 2))
    if fmt == "e4m3":
        words = by_word.astype(ml_dtypes.float8_e4m3fn).view(np.uint8)
    else:
        c = by_word.astype(ml_dtypes.float4_e2m1fn).view(np.uint8) & 0xF
        words = c[..., 0::2] | (c[..., 1::2] << 4)
    return np.ascontiguousarray(words), np.ascontiguousarray(byte.astype(np.uint8).reshape(k // 512, 16, n))


def unpack_weight(words, scales, fmt):
    g, p, n, _ = words.shape
    if fmt == "e4m3":
        vals = np.ascontiguousarray(words).view(ml_dtypes.float8_e4m3fn).astype(np.float64)
    else:
        nib = np.empty((g, p, n, 4), np.uint8)
        nib[..., 0::2] = words & 0xF
        nib[..., 1::2] = words >> 4
        vals = E2M1[nib]
    vals = vals * np.repeat(np.exp2(scales.astype(np.float64) - 127.0), 8, axis=1)[..., None]
    return vals.transpose(0, 1, 3, 2).reshape(g * 512, n)


G, D1, D2, D3, K, N = 16, 2, 8, 8, 512, 512

EPS = 1e-6


def setup_inputs():
    s = mx_kscale(K)
    rows = np.random.standard_normal((G, D1, D2, D3, K))
    rows = rows * (0.5 + 1.5 * np.random.random_sample((G, D1, D2, D3, 1))) + 0.5 * np.random.standard_normal((G, D1, D2, D3, 1))
    x = bf(rows.reshape(G * K, D1, D2, D3))
    ln_gamma = bf((1.0 + 0.1 * np.random.standard_normal((G, K))) * s)
    ln_beta = bf(0.1 * np.random.standard_normal((G, K)) * s)
    stack = (np.random.standard_normal((G, N, K)) / np.sqrt(K) / s).swapaxes(1, 2)
    words, scales = pack_weight(stack.reshape(-1, N), "e4m3")
    b = bf(0.1 * np.random.standard_normal((G, N)))
    return {"x": x,
            "ln_gamma": ln_gamma,
            "ln_beta": ln_beta,
            "W_words": words,
            "W_scales": scales,
            "b": b}


def reference(x, ln_gamma, ln_beta, W_words, W_scales, b):
    xg = f64(x).reshape(G, D1, D2, D3, K)
    mu = np.mean(xg, axis=-1, keepdims=True)
    var = np.mean(np.square(xg - mu), axis=-1, keepdims=True)
    xn = (xg - mu) / np.sqrt(var + EPS)
    xn = xn * f64(ln_gamma)[:, None, None, None, :] + f64(ln_beta)[:, None, None, None, :]
    a = mxq(xn.reshape(G, D1 * D2 * D3, K), 2, "e4m3")
    y = a @ unpack_weight(W_words, W_scales, "e4m3").reshape(G, K, N)
    y = y.reshape(G, D1, D2, D3, N) + f64(b)[:, None, None, None, :]
    y = np.moveaxis(y, 0, -2).reshape(D1, D2, D3, G * N)
    return np.transpose(y, (3, 0, 1, 2))

@@ -1,0 +1,165 @@
+from contextlib import ExitStack
+
+import concourse.mybir as mybir
+from concourse.masks import make_identity
+
+F32 = mybir.dt.float32
+BF16 = mybir.dt.bfloat16
+I32 = mybir.dt.int32
+U32 = mybir.dt.uint32
+U8 = mybir.dt.uint8
+FP8X4 = mybir.dt.float8_e4m3fn_x4
+ACT = mybir.ActivationFunctionType
+ALU = mybir.AluOpType
+
+P = 128
+PACK = 4
+GROUPS = 16
+ROWS = 128
+K = 512
+N_OUT = 512
+O_TILES = N_OUT // P
+CHUNK = 4
+CHUNKS = GROUPS // CHUNK
+EPS = 1e-6
+BN_STATS_DIM = 6
+QUADRANT = 32
+
+FLOPS = 2 * GROUPS * ROWS * K * N_OUT
+
+
+def tile_groupedlinear_e_kernel(tc, x, ln_gamma, ln_beta, W_words, W_scales, b, out):
+    nc = tc.nc
+
+    x_rows = x.rearrange("(g r c) h i j -> r g (c h i j)", g=GROUPS, r=ROWS)
+    w_words_hbm = W_words.rearrange("g p n t -> p g (n t)").bitcast(I32)
+    w_scales_hbm = W_scales.bitcast(I32)
+    out_rows = out.rearrange("(g c m) h i j -> m g c (h i j)", g=GROUPS, c=O_TILES)
+
+    with ExitStack() as ctx:
+        keep = ctx.enter_context(tc.tile_pool(name="keep", bufs=1))
+        work = ctx.enter_context(tc.tile_pool(name="work", bufs=4))
+        psum_t = ctx.enter_context(tc.psum_pool(name="psum_t", bufs=4))
+        psum_y = ctx.enter_context(tc.psum_pool(name="psum_y", bufs=4))
+
+        x_sb = keep.tile([P, GROUPS, K], BF16)
+        w_sb = keep.tile([P, GROUPS, N_OUT], I32, align_bytes=64)
+        w_planes = keep.tile([P, CHUNKS, N_OUT], U8, align_bytes=64)
+        xn_codes = keep.tile([P, GROUPS, ROWS], U32, align_bytes=64)
+        xn_planes = keep.tile([P, GROUPS, ROWS], U8, align_bytes=64)
+
+        nc.vector.memset(w_planes[:].bitcast(I32), 0)
+        for a in range(CHUNKS):
+            groups = slice(a * CHUNK, (a + 1) * CHUNK)
+            nc.sync.dma_start(out=x_sb[:, groups, :], in_=x_rows[:, groups, :])
+        for a in range(CHUNKS):
+            for quad in range(P // QUADRANT):
+                nc.sync.dma_start(
+                    out=w_planes[quad * QUADRANT : quad * QUADRANT + 4 * CHUNK, a, :].bitcast(I32),
+                    in_=w_scales_hbm[a * CHUNK : (a + 1) * CHUNK, 4 * quad : 4 * quad + 4, :],
+                )
+        for a in range(CHUNKS):
+            groups = slice(a * CHUNK, (a + 1) * CHUNK)
+            nc.sync.dma_start(out=w_sb[:, groups, :], in_=w_words_hbm[:, groups, :])
+
+        ident = keep.tile([P, P], F32)
+        make_identity(nc, ident[:])
+        par_rows = keep.tile([P, K], BF16)
+        nc.vector.memset(par_rows[:], 0.0)
+        nc.scalar.dma_start(out=par_rows[0:GROUPS, :], in_=ln_gamma)
+        nc.scalar.dma_start(out=par_rows[GROUPS : 2 * GROUPS, :], in_=ln_beta)
+        nc.scalar.dma_start(out=par_rows[2 * GROUPS : 3 * GROUPS, :], in_=b)
+        par_by_t = keep.tile([P, PACK, P], F32)
+        nc.vector.tensor_copy(out=par_by_t[:], in_=par_rows[:].rearrange("r (p t) -> r t p", t=PACK))
+        par_by_c = keep.tile([P, O_TILES, P], F32)
+        nc.vector.tensor_copy(out=par_by_c[:], in_=par_rows[:].rearrange("r (c m) -> r c m", c=O_TILES))
+        par_t_ps = psum_t.tile([P, PACK, P], F32, tag="transposed")
+        par_c_ps = psum_t.tile([P, O_TILES, P], F32, tag="transposed")
+        for t in range(PACK):
+            nc.tensor.transpose(par_t_ps[:, t, :], par_by_t[:, t, :], ident[:])
+        for c in range(O_TILES):
+            nc.tensor.transpose(par_c_ps[:, c, :], par_by_c[:, c, :], ident[:])
+        gamma_beta = keep.tile([P, PACK, 2 * GROUPS], F32)
+        nc.vector.tensor_copy(out=gamma_beta[:], in_=par_t_ps[:, :, 0 : 2 * GROUPS])
+        bias_cols = keep.tile([P, O_TILES, GROUPS], F32)
+        nc.vector.tensor_copy(out=bias_cols[:], in_=par_c_ps[:, :, 2 * GROUPS : 3 * GROUPS])
+
+        eps_col = keep.tile([P, 1], F32)
+        nc.vector.memset(eps_col[:], EPS)
+        stats = keep.tile([P, GROUPS, BN_STATS_DIM], F32)
+        mean_var = keep.tile([P, GROUPS, 2], F32)
+        std = keep.tile([P, GROUPS], F32)
+        rstd = keep.tile([P, GROUPS], F32)
+
+        def row_statistics(a):
+            groups = slice(a * CHUNK, (a + 1) * CHUNK)
+            for g in range(a * CHUNK, (a + 1) * CHUNK):
+                nc.vector.bn_stats(out=stats[:, g, :], in_=x_sb[:, g, :])
+                nc.vector.bn_aggr(out=mean_var[:, g, :], in_=stats[:, g, :])
+            nc.scalar.activation(
+                out=std[:, groups], in_=mean_var[:, groups, 1], func=ACT.Sqrt, bias=eps_col[:], scale=1.0
+            )
+            nc.vector.reciprocal(out=rstd[:, groups], in_=std[:, groups])
+
+        def quantise_group(g):
+            z = work.tile([P, PACK, P], F32)
+            nc.vector.tensor_scalar(
+                out=z[:],
+                in0=x_sb[:, g, :].rearrange("r (p t) -> r t p", t=PACK),
+                scalar1=mean_var[:, g, 0:1],
+                scalar2=rstd[:, g : g + 1],
+                op0=ALU.subtract,
+                op1=ALU.mult,
+            )
+            z_t = psum_t.tile([P, PACK, ROWS], F32, tag="transposed")
+            for t in range(PACK):
+                nc.tensor.transpose(z_t[:, t, :], z[:, t, :], ident[:])
+            xn_by_t = work.tile([P, PACK, ROWS], BF16)
+            for t in range(PACK):
+                nc.scalar.activation(
+                    out=xn_by_t[:, t, :],
+                    in_=z_t[:, t, :],
+                    func=ACT.Identity,
+                    scale=gamma_beta[:, t, g : g + 1],
+                    bias=gamma_beta[:, t, GROUPS + g : GROUPS + g + 1],
+                )
+            xn_words = work.tile([P, ROWS, PACK], BF16, align_bytes=64)
+            nc.vector.tensor_copy(out=xn_words[:], in_=xn_by_t[:].rearrange("p t r -> p r t"))
+            nc.vector.quantize_mx(
+                out=xn_codes[:, g, :].bitcast(FP8X4),
+                scales=xn_planes[:, g, :],
+                in_=xn_words[:].rearrange("p r t -> p (r t)"),
+            )
+
+        def multiply_group(g):
+            a = g // CHUNK
+            first_row = PACK * (g % CHUNK)
+            y_ps = psum_y.tile([P, O_TILES, ROWS], F32)
+            for c in range(O_TILES):
+                cols = slice(c * P, (c + 1) * P)
+                nc.tensor.matmul_mx(
+                    out=y_ps[:, c, :],
+                    lhsT=w_sb[:, g, cols].bitcast(FP8X4),
+                    lhsT_scale=w_planes[first_row:P, a, cols],
+                    rhs=xn_codes[:, g, :].bitcast(FP8X4),
+                    rhs_scale=xn_planes[:, g, :],
+                    start=True,
+                    stop=True,
+                )
+            y_sb = work.tile([P, O_TILES, ROWS], F32)
+            for c in range(O_TILES):
+                nc.scalar.activation(
+                    out=y_sb[:, c, :],
+                    in_=y_ps[:, c, :],
+                    func=ACT.Identity,
+                    bias=bias_cols[:, c, g : g + 1],
+                    scale=1.0,
+                )
+            nc.sync.dma_start(out=out_rows[:, g, :, :], in_=y_sb[:])
+
+        for a in range(CHUNKS):
+            row_statistics(a)
+            for g in range(a * CHUNK, (a + 1) * CHUNK):
+                quantise_group(g)
+            for g in range(a * CHUNK, (a + 1) * CHUNK):
+                multiply_group(g)

@@ -19,11 +19,14 @@ ROWS = 128
 K = 512
 N_OUT = 512
 O_TILES = N_OUT // P
-CHUNK = 4
-CHUNKS = GROUPS // CHUNK
 EPS = 1e-6
 BN_STATS_DIM = 6
 QUADRANT = 32
+PLANES = 4
+PAIR = 2
+W_CHUNK = 4
+VECTOR_SHARE = 3
+LIVE = 4
 
 FLOPS = 2 * GROUPS * ROWS * K * N_OUT
 
@@ -38,37 +41,43 @@ def tile_groupedlinear_e_kernel(tc, x, ln_gamma, ln_beta, W_words, W_scales, b, 
 
     with ExitStack() as ctx:
         keep = ctx.enter_context(tc.tile_pool(name="keep", bufs=1))
-        work = ctx.enter_context(tc.tile_pool(name="work", bufs=4))
-        psum_t = ctx.enter_context(tc.psum_pool(name="psum_t", bufs=4))
-        psum_y = ctx.enter_context(tc.psum_pool(name="psum_y", bufs=4))
+        work = ctx.enter_context(tc.tile_pool(name="work", bufs=LIVE))
+        psum_t = ctx.enter_context(tc.psum_pool(name="psum_t", bufs=LIVE))
+        psum_y = ctx.enter_context(tc.psum_pool(name="psum_y", bufs=LIVE))
 
         x_sb = keep.tile([P, GROUPS, K], BF16)
         w_sb = keep.tile([P, GROUPS, N_OUT], I32, align_bytes=64)
-        w_planes = keep.tile([P, CHUNKS, N_OUT], U8, align_bytes=64)
+        w_planes = keep.tile([P, GROUPS // PLANES, N_OUT], U8, align_bytes=64)
         xn_codes = keep.tile([P, GROUPS, ROWS], U32, align_bytes=64)
         xn_planes = keep.tile([P, GROUPS, ROWS], U8, align_bytes=64)
+        y_sb = keep.tile([P, GROUPS, O_TILES, ROWS], F32)
+        par_rows = keep.tile([P, K], BF16)
 
+        nc.vector.memset(par_rows[:], 0.0)
         nc.vector.memset(w_planes[:].bitcast(I32), 0)
-        for a in range(CHUNKS):
-            groups = slice(a * CHUNK, (a + 1) * CHUNK)
-            nc.sync.dma_start(out=x_sb[:, groups, :], in_=x_rows[:, groups, :])
-        for a in range(CHUNKS):
+        for first in range(0, GROUPS, PAIR):
+            nc.sync.dma_start(out=x_sb[:, first : first + PAIR, :], in_=x_rows[:, first : first + PAIR, :])
+        for a in range(GROUPS // PLANES):
             for quad in range(P // QUADRANT):
                 nc.sync.dma_start(
-                    out=w_planes[quad * QUADRANT : quad * QUADRANT + 4 * CHUNK, a, :].bitcast(I32),
-                    in_=w_scales_hbm[a * CHUNK : (a + 1) * CHUNK, 4 * quad : 4 * quad + 4, :],
+                    out=w_planes[quad * QUADRANT : quad * QUADRANT + 4 * PLANES, a, :].bitcast(I32),
+                    in_=w_scales_hbm[a * PLANES : (a + 1) * PLANES, 4 * quad : 4 * quad + 4, :],
                 )
-        for a in range(CHUNKS):
-            groups = slice(a * CHUNK, (a + 1) * CHUNK)
-            nc.sync.dma_start(out=w_sb[:, groups, :], in_=w_words_hbm[:, groups, :])
+        for first in range(0, GROUPS, W_CHUNK):
+            nc.sync.dma_start(
+                out=w_sb[:, first : first + W_CHUNK, :], in_=w_words_hbm[:, first : first + W_CHUNK, :]
+            )
 
-        ident = keep.tile([P, P], F32)
-        make_identity(nc, ident[:])
-        par_rows = keep.tile([P, K], BF16)
-        nc.vector.memset(par_rows[:], 0.0)
+        eps_col = keep.tile([P, 1], F32)
+        nc.vector.memset(eps_col[:], EPS)
+        first_sqrt = keep.tile([P, 1], F32)
+        nc.scalar.activation(out=first_sqrt[:], in_=eps_col[:], func=ACT.Sqrt)
+
         nc.scalar.dma_start(out=par_rows[0:GROUPS, :], in_=ln_gamma)
         nc.scalar.dma_start(out=par_rows[GROUPS : 2 * GROUPS, :], in_=ln_beta)
         nc.scalar.dma_start(out=par_rows[2 * GROUPS : 3 * GROUPS, :], in_=b)
+        ident = keep.tile([P, P], F32)
+        make_identity(nc, ident[:])
         par_by_t = keep.tile([P, PACK, P], F32)
         nc.vector.tensor_copy(out=par_by_t[:], in_=par_rows[:].rearrange("r (p t) -> r t p", t=PACK))
         par_by_c = keep.tile([P, O_TILES, P], F32)
@@ -80,35 +89,35 @@ def tile_groupedlinear_e_kernel(tc, x, ln_gamma, ln_beta, W_words, W_scales, b, 
         for c in range(O_TILES):
             nc.tensor.transpose(par_c_ps[:, c, :], par_by_c[:, c, :], ident[:])
         gamma_beta = keep.tile([P, PACK, 2 * GROUPS], F32)
-        nc.vector.tensor_copy(out=gamma_beta[:], in_=par_t_ps[:, :, 0 : 2 * GROUPS])
+        nc.scalar.copy(out=gamma_beta[:], in_=par_t_ps[:, :, 0 : 2 * GROUPS])
         bias_cols = keep.tile([P, O_TILES, GROUPS], F32)
-        nc.vector.tensor_copy(out=bias_cols[:], in_=par_c_ps[:, :, 2 * GROUPS : 3 * GROUPS])
+        nc.scalar.copy(out=bias_cols[:], in_=par_c_ps[:, :, 2 * GROUPS : 3 * GROUPS])
 
-        eps_col = keep.tile([P, 1], F32)
-        nc.vector.memset(eps_col[:], EPS)
         stats = keep.tile([P, GROUPS, BN_STATS_DIM], F32)
         mean_var = keep.tile([P, GROUPS, 2], F32)
+        neg_mean = keep.tile([P, GROUPS], F32)
         std = keep.tile([P, GROUPS], F32)
         rstd = keep.tile([P, GROUPS], F32)
 
-        def row_statistics(a):
-            groups = slice(a * CHUNK, (a + 1) * CHUNK)
-            for g in range(a * CHUNK, (a + 1) * CHUNK):
+        def row_statistics(first):
+            groups = slice(first, first + PAIR)
+            for g in range(first, first + PAIR):
                 nc.vector.bn_stats(out=stats[:, g, :], in_=x_sb[:, g, :])
                 nc.vector.bn_aggr(out=mean_var[:, g, :], in_=stats[:, g, :])
             nc.scalar.activation(
                 out=std[:, groups], in_=mean_var[:, groups, 1], func=ACT.Sqrt, bias=eps_col[:], scale=1.0
             )
+            nc.vector.tensor_scalar_mul(out=neg_mean[:, groups], in0=mean_var[:, groups, 0], scalar1=-1.0)
             nc.vector.reciprocal(out=rstd[:, groups], in_=std[:, groups])
 
         def quantise_group(g):
             z = work.tile([P, PACK, P], F32)
-            nc.vector.tensor_scalar(
+            nc.gpsimd.tensor_scalar(
                 out=z[:],
                 in0=x_sb[:, g, :].rearrange("r (p t) -> r t p", t=PACK),
-                scalar1=mean_var[:, g, 0:1],
+                scalar1=neg_mean[:, g : g + 1],
                 scalar2=rstd[:, g : g + 1],
-                op0=ALU.subtract,
+                op0=ALU.add,
                 op1=ALU.mult,
             )
             z_t = psum_t.tile([P, PACK, ROWS], F32, tag="transposed")
@@ -132,8 +141,8 @@ def tile_groupedlinear_e_kernel(tc, x, ln_gamma, ln_beta, W_words, W_scales, b, 
             )
 
         def multiply_group(g):
-            a = g // CHUNK
-            first_row = PACK * (g % CHUNK)
+            a = g // PLANES
+            first_row = 4 * (g % PLANES)
             y_ps = psum_y.tile([P, O_TILES, ROWS], F32)
             for c in range(O_TILES):
                 cols = slice(c * P, (c + 1) * P)
@@ -146,20 +155,27 @@ def tile_groupedlinear_e_kernel(tc, x, ln_gamma, ln_beta, W_words, W_scales, b, 
                     start=True,
                     stop=True,
                 )
-            y_sb = work.tile([P, O_TILES, ROWS], F32)
-            for c in range(O_TILES):
-                nc.scalar.activation(
-                    out=y_sb[:, c, :],
-                    in_=y_ps[:, c, :],
-                    func=ACT.Identity,
-                    bias=bias_cols[:, c, g : g + 1],
-                    scale=1.0,
+            if g % VECTOR_SHARE == 0:
+                nc.vector.tensor_tensor(
+                    out=y_sb[:, g, :, :],
+                    in0=y_ps[:],
+                    in1=bias_cols[:, :, g : g + 1].to_broadcast([P, O_TILES, ROWS]),
+                    op=ALU.add,
                 )
-            nc.sync.dma_start(out=out_rows[:, g, :, :], in_=y_sb[:])
+            else:
+                for c in range(O_TILES):
+                    nc.scalar.activation(
+                        out=y_sb[:, g, c, :],
+                        in_=y_ps[:, c, :],
+                        func=ACT.Identity,
+                        bias=bias_cols[:, c, g : g + 1],
+                        scale=1.0,
+                    )
+            nc.sync.dma_start(out=out_rows[:, g, :, :], in_=y_sb[:, g, :, :])
 
-        for a in range(CHUNKS):
-            row_statistics(a)
-            for g in range(a * CHUNK, (a + 1) * CHUNK):
+        for first in range(0, GROUPS, PAIR):
+            row_statistics(first)
+            for g in range(first, first + PAIR):
                 quantise_group(g)
-            for g in range(a * CHUNK, (a + 1) * CHUNK):
+            for g in range(first, first + PAIR):
                 multiply_group(g)

@@ -25,6 +25,9 @@ QUADRANT = 32
 PLANES = 4
 PAIR = 2
 W_CHUNK = 4
+
+STAGE_LAG = 2
+STATS_AHEAD = 3
 VECTOR_SHARE = 3
 LIVE = 4
 
@@ -44,6 +47,7 @@ def tile_groupedlinear_e_kernel(tc, x, ln_gamma, ln_beta, W_words, W_scales, b, 
         work = ctx.enter_context(tc.tile_pool(name="work", bufs=LIVE))
         psum_t = ctx.enter_context(tc.psum_pool(name="psum_t", bufs=LIVE))
         psum_y = ctx.enter_context(tc.psum_pool(name="psum_y", bufs=LIVE))
+        ctx.enter_context(tc.manual_schedule())
 
         x_sb = keep.tile([P, GROUPS, K], BF16)
         w_sb = keep.tile([P, GROUPS, N_OUT], I32, align_bytes=64)
@@ -79,9 +83,23 @@ def tile_groupedlinear_e_kernel(tc, x, ln_gamma, ln_beta, W_words, W_scales, b, 
         ident = keep.tile([P, P], F32)
         make_identity(nc, ident[:])
         par_by_t = keep.tile([P, PACK, P], F32)
-        nc.vector.tensor_copy(out=par_by_t[:], in_=par_rows[:].rearrange("r (p t) -> r t p", t=PACK))
+        nc.gpsimd.tensor_scalar(
+            out=par_by_t[:],
+            in0=par_rows[:].rearrange("r (p t) -> r t p", t=PACK),
+            scalar1=1.0,
+            scalar2=0.0,
+            op0=ALU.mult,
+            op1=ALU.add,
+        )
         par_by_c = keep.tile([P, O_TILES, P], F32)
-        nc.vector.tensor_copy(out=par_by_c[:], in_=par_rows[:].rearrange("r (c m) -> r c m", c=O_TILES))
+        nc.gpsimd.tensor_scalar(
+            out=par_by_c[:],
+            in0=par_rows[:].rearrange("r (c m) -> r c m", c=O_TILES),
+            scalar1=1.0,
+            scalar2=0.0,
+            op0=ALU.mult,
+            op1=ALU.add,
+        )
         par_t_ps = psum_t.tile([P, PACK, P], F32, tag="transposed")
         par_c_ps = psum_t.tile([P, O_TILES, P], F32, tag="transposed")
         for t in range(PACK):
@@ -89,28 +107,36 @@ def tile_groupedlinear_e_kernel(tc, x, ln_gamma, ln_beta, W_words, W_scales, b, 
         for c in range(O_TILES):
             nc.tensor.transpose(par_c_ps[:, c, :], par_by_c[:, c, :], ident[:])
         gamma_beta = keep.tile([P, PACK, 2 * GROUPS], F32)
-        nc.scalar.copy(out=gamma_beta[:], in_=par_t_ps[:, :, 0 : 2 * GROUPS])
         bias_cols = keep.tile([P, O_TILES, GROUPS], F32)
-        nc.scalar.copy(out=bias_cols[:], in_=par_c_ps[:, :, 2 * GROUPS : 3 * GROUPS])
+
+        def keep_parameters():
+            nc.scalar.copy(out=gamma_beta[:], in_=par_t_ps[:, :, 0 : 2 * GROUPS])
+            nc.scalar.copy(out=bias_cols[:], in_=par_c_ps[:, :, 2 * GROUPS : 3 * GROUPS])
 
         stats = keep.tile([P, GROUPS, BN_STATS_DIM], F32)
         mean_var = keep.tile([P, GROUPS, 2], F32)
-        neg_mean = keep.tile([P, GROUPS], F32)
         std = keep.tile([P, GROUPS], F32)
         rstd = keep.tile([P, GROUPS], F32)
+        neg_mean = keep.tile([P, GROUPS], F32)
+        z_t_of = {}
+        xn_by_t_of = {}
+        xn_words_of = {}
+        y_ps_of = {}
 
-        def row_statistics(first):
-            groups = slice(first, first + PAIR)
-            for g in range(first, first + PAIR):
-                nc.vector.bn_stats(out=stats[:, g, :], in_=x_sb[:, g, :])
-                nc.vector.bn_aggr(out=mean_var[:, g, :], in_=stats[:, g, :])
+        def mean_and_variance(g):
+            nc.vector.bn_stats(out=stats[:, g, :], in_=x_sb[:, g, :])
+            nc.vector.bn_aggr(out=mean_var[:, g, :], in_=stats[:, g, :])
+
+        def standard_deviation(groups):
             nc.scalar.activation(
                 out=std[:, groups], in_=mean_var[:, groups, 1], func=ACT.Sqrt, bias=eps_col[:], scale=1.0
             )
-            nc.vector.tensor_scalar_mul(out=neg_mean[:, groups], in0=mean_var[:, groups, 0], scalar1=-1.0)
-            nc.vector.reciprocal(out=rstd[:, groups], in_=std[:, groups])
 
-        def quantise_group(g):
+        def scale_and_shift_of_rows(groups):
+            nc.vector.reciprocal(out=rstd[:, groups], in_=std[:, groups])
+            nc.vector.tensor_scalar_mul(out=neg_mean[:, groups], in0=mean_var[:, groups, 0], scalar1=-1.0)
+
+        def normalise(g):
             z = work.tile([P, PACK, P], F32)
             nc.gpsimd.tensor_scalar(
                 out=z[:],
@@ -123,24 +149,33 @@ def tile_groupedlinear_e_kernel(tc, x, ln_gamma, ln_beta, W_words, W_scales, b, 
             z_t = psum_t.tile([P, PACK, ROWS], F32, tag="transposed")
             for t in range(PACK):
                 nc.tensor.transpose(z_t[:, t, :], z[:, t, :], ident[:])
+            z_t_of[g] = z_t
+
+        def scale_shift(g):
             xn_by_t = work.tile([P, PACK, ROWS], BF16)
             for t in range(PACK):
                 nc.scalar.activation(
                     out=xn_by_t[:, t, :],
-                    in_=z_t[:, t, :],
+                    in_=z_t_of[g][:, t, :],
                     func=ACT.Identity,
                     scale=gamma_beta[:, t, g : g + 1],
                     bias=gamma_beta[:, t, GROUPS + g : GROUPS + g + 1],
                 )
+            xn_by_t_of[g] = xn_by_t
+
+        def regroup(g):
             xn_words = work.tile([P, ROWS, PACK], BF16, align_bytes=64)
-            nc.vector.tensor_copy(out=xn_words[:], in_=xn_by_t[:].rearrange("p t r -> p r t"))
+            nc.vector.tensor_copy(out=xn_words[:], in_=xn_by_t_of[g][:].rearrange("p t r -> p r t"))
+            xn_words_of[g] = xn_words
+
+        def quantise(g):
             nc.vector.quantize_mx(
                 out=xn_codes[:, g, :].bitcast(FP8X4),
                 scales=xn_planes[:, g, :],
-                in_=xn_words[:].rearrange("p r t -> p (r t)"),
+                in_=xn_words_of[g][:].rearrange("p r t -> p (r t)"),
             )
 
-        def multiply_group(g):
+        def multiply(g):
             a = g // PLANES
             first_row = 4 * (g % PLANES)
             y_ps = psum_y.tile([P, O_TILES, ROWS], F32)
@@ -155,10 +190,13 @@ def tile_groupedlinear_e_kernel(tc, x, ln_gamma, ln_beta, W_words, W_scales, b, 
                     start=True,
                     stop=True,
                 )
+            y_ps_of[g] = y_ps
+
+        def add_bias_and_store(g):
             if g % VECTOR_SHARE == 0:
                 nc.vector.tensor_tensor(
                     out=y_sb[:, g, :, :],
-                    in0=y_ps[:],
+                    in0=y_ps_of[g][:],
                     in1=bias_cols[:, :, g : g + 1].to_broadcast([P, O_TILES, ROWS]),
                     op=ALU.add,
                 )
@@ -166,16 +204,39 @@ def tile_groupedlinear_e_kernel(tc, x, ln_gamma, ln_beta, W_words, W_scales, b, 
                 for c in range(O_TILES):
                     nc.scalar.activation(
                         out=y_sb[:, g, c, :],
-                        in_=y_ps[:, c, :],
+                        in_=y_ps_of[g][:, c, :],
                         func=ACT.Identity,
                         bias=bias_cols[:, c, g : g + 1],
                         scale=1.0,
                     )
             nc.sync.dma_start(out=out_rows[:, g, :, :], in_=y_sb[:, g, :, :])
 
-        for first in range(0, GROUPS, PAIR):
-            row_statistics(first)
-            for g in range(first, first + PAIR):
-                quantise_group(g)
-            for g in range(first, first + PAIR):
-                multiply_group(g)
+        def is_group(g):
+            return 0 <= g < GROUPS
+
+        for tick in range(-STATS_AHEAD, GROUPS + 4 * STAGE_LAG):
+            g_stats = tick + STATS_AHEAD
+            g_scale = tick - STAGE_LAG
+            g_pack = tick - 2 * STAGE_LAG
+            g_multiply = tick - 3 * STAGE_LAG
+            g_store = tick - 4 * STAGE_LAG
+            if is_group(g_pack):
+                regroup(g_pack)
+            if is_group(g_stats):
+                mean_and_variance(g_stats)
+            if is_group(g_pack):
+                quantise(g_pack)
+            if is_group(g_stats - 1) and g_stats % PAIR == 0:
+                scale_and_shift_of_rows(slice(g_stats - PAIR, g_stats))
+            if is_group(tick):
+                normalise(tick)
+            if g_scale == 0:
+                keep_parameters()
+            if is_group(g_scale):
+                scale_shift(g_scale)
+            if is_group(g_multiply):
+                multiply(g_multiply)
+            if is_group(g_store):
+                add_bias_and_store(g_store)
+            if is_group(g_stats) and g_stats % PAIR == PAIR - 1:
+                standard_deviation(slice(g_stats + 1 - PAIR, g_stats + 1))

@@ -24,7 +24,6 @@ BN_STATS_DIM = 6
 QUADRANT = 32
 PLANES = 4
 PAIR = 2
-W_CHUNK = 4
 
 STAGE_LAG = 2
 STATS_AHEAD = 3
@@ -62,15 +61,13 @@ def tile_groupedlinear_e_kernel(tc, x, ln_gamma, ln_beta, W_words, W_scales, b, 
         for first in range(0, GROUPS, PAIR):
             nc.sync.dma_start(out=x_sb[:, first : first + PAIR, :], in_=x_rows[:, first : first + PAIR, :])
         for a in range(GROUPS // PLANES):
+            groups = slice(a * PLANES, (a + 1) * PLANES)
             for quad in range(P // QUADRANT):
                 nc.sync.dma_start(
                     out=w_planes[quad * QUADRANT : quad * QUADRANT + 4 * PLANES, a, :].bitcast(I32),
-                    in_=w_scales_hbm[a * PLANES : (a + 1) * PLANES, 4 * quad : 4 * quad + 4, :],
+                    in_=w_scales_hbm[groups, 4 * quad : 4 * quad + 4, :],
                 )
-        for first in range(0, GROUPS, W_CHUNK):
-            nc.sync.dma_start(
-                out=w_sb[:, first : first + W_CHUNK, :], in_=w_words_hbm[:, first : first + W_CHUNK, :]
-            )
+            nc.sync.dma_start(out=w_sb[:, groups, :], in_=w_words_hbm[:, groups, :])
 
         eps_col = keep.tile([P, 1], F32)
         nc.vector.memset(eps_col[:], EPS)

@@ -23,11 +23,9 @@ EPS = 1e-6
 BN_STATS_DIM = 6
 QUADRANT = 32
 PLANES = 4
-PAIR = 2
 
-STAGE_LAG = 2
-STATS_AHEAD = 3
-VECTOR_SHARE = 3
+STATS_AHEAD = 2
+VECTOR_TAIL = 2
 LIVE = 4
 
 FLOPS = 2 * GROUPS * ROWS * K * N_OUT
@@ -55,12 +53,20 @@ def tile_groupedlinear_e_kernel(tc, x, ln_gamma, ln_beta, W_words, W_scales, b, 
         xn_planes = keep.tile([P, GROUPS, ROWS], U8, align_bytes=64)
         y_sb = keep.tile([P, GROUPS, O_TILES, ROWS], F32)
         par_rows = keep.tile([P, K], BF16)
+        eps_col = keep.tile([P, 1], F32)
 
         nc.vector.memset(par_rows[:], 0.0)
+        nc.vector.memset(eps_col[:], EPS)
         nc.vector.memset(w_planes[:].bitcast(I32), 0)
-        for first in range(0, GROUPS, PAIR):
-            nc.sync.dma_start(out=x_sb[:, first : first + PAIR, :], in_=x_rows[:, first : first + PAIR, :])
-        for a in range(GROUPS // PLANES):
+
+        nc.scalar.dma_start(out=par_rows[0:GROUPS, :], in_=ln_gamma)
+        nc.scalar.dma_start(out=par_rows[GROUPS : 2 * GROUPS, :], in_=ln_beta)
+        nc.scalar.dma_start(out=par_rows[2 * GROUPS : 3 * GROUPS, :], in_=b)
+
+        def load_x(first, count):
+            nc.sync.dma_start(out=x_sb[:, first : first + count, :], in_=x_rows[:, first : first + count, :])
+
+        def load_weight(a):
             groups = slice(a * PLANES, (a + 1) * PLANES)
             for quad in range(P // QUADRANT):
                 nc.sync.dma_start(
@@ -69,42 +75,39 @@ def tile_groupedlinear_e_kernel(tc, x, ln_gamma, ln_beta, W_words, W_scales, b, 
                 )
             nc.sync.dma_start(out=w_sb[:, groups, :], in_=w_words_hbm[:, groups, :])
 
-        eps_col = keep.tile([P, 1], F32)
-        nc.vector.memset(eps_col[:], EPS)
-        first_sqrt = keep.tile([P, 1], F32)
-        nc.scalar.activation(out=first_sqrt[:], in_=eps_col[:], func=ACT.Sqrt)
+        load_x(0, 1)
+        load_x(1, 1)
+        load_x(2, 2)
+        load_x(4, 4)
+        load_weight(0)
+        load_x(8, 4)
+        load_x(12, 4)
+        load_weight(1)
+        load_weight(2)
+        load_weight(3)
 
-        nc.scalar.dma_start(out=par_rows[0:GROUPS, :], in_=ln_gamma)
-        nc.scalar.dma_start(out=par_rows[GROUPS : 2 * GROUPS, :], in_=ln_beta)
-        nc.scalar.dma_start(out=par_rows[2 * GROUPS : 3 * GROUPS, :], in_=b)
+        first_rstd = keep.tile([P, 1], F32)
+        nc.scalar.activation(out=first_rstd[:], in_=eps_col[:], func=ACT.Abs_reciprocal_sqrt)
+
         ident = keep.tile([P, P], F32)
         make_identity(nc, ident[:])
+
         par_by_t = keep.tile([P, PACK, P], F32)
-        nc.gpsimd.tensor_scalar(
-            out=par_by_t[:],
-            in0=par_rows[:].rearrange("r (p t) -> r t p", t=PACK),
-            scalar1=1.0,
-            scalar2=0.0,
-            op0=ALU.mult,
-            op1=ALU.add,
-        )
         par_by_c = keep.tile([P, O_TILES, P], F32)
-        nc.gpsimd.tensor_scalar(
-            out=par_by_c[:],
-            in0=par_rows[:].rearrange("r (c m) -> r c m", c=O_TILES),
-            scalar1=1.0,
-            scalar2=0.0,
-            op0=ALU.mult,
-            op1=ALU.add,
-        )
         par_t_ps = psum_t.tile([P, PACK, P], F32, tag="transposed")
         par_c_ps = psum_t.tile([P, O_TILES, P], F32, tag="transposed")
-        for t in range(PACK):
-            nc.tensor.transpose(par_t_ps[:, t, :], par_by_t[:, t, :], ident[:])
-        for c in range(O_TILES):
-            nc.tensor.transpose(par_c_ps[:, c, :], par_by_c[:, c, :], ident[:])
         gamma_beta = keep.tile([P, PACK, 2 * GROUPS], F32)
         bias_cols = keep.tile([P, O_TILES, GROUPS], F32)
+
+        def widen_gamma_beta():
+            nc.scalar.activation(out=par_by_t[:], in_=par_rows[:].rearrange("r (p t) -> r t p", t=PACK), func=ACT.Copy)
+            for t in range(PACK):
+                nc.tensor.transpose(par_t_ps[:, t, :], par_by_t[:, t, :], ident[:])
+
+        def widen_bias():
+            nc.scalar.activation(out=par_by_c[:], in_=par_rows[:].rearrange("r (c m) -> r c m", c=O_TILES), func=ACT.Copy)
+            for c in range(O_TILES):
+                nc.tensor.transpose(par_c_ps[:, c, :], par_by_c[:, c, :], ident[:])
 
         def keep_parameters():
             nc.scalar.copy(out=gamma_beta[:], in_=par_t_ps[:, :, 0 : 2 * GROUPS])
@@ -112,37 +115,40 @@ def tile_groupedlinear_e_kernel(tc, x, ln_gamma, ln_beta, W_words, W_scales, b, 
 
         stats = keep.tile([P, GROUPS, BN_STATS_DIM], F32)
         mean_var = keep.tile([P, GROUPS, 2], F32)
-        std = keep.tile([P, GROUPS], F32)
         rstd = keep.tile([P, GROUPS], F32)
-        neg_mean = keep.tile([P, GROUPS], F32)
         z_t_of = {}
         xn_by_t_of = {}
         xn_words_of = {}
         y_ps_of = {}
 
-        def mean_and_variance(g):
+        def sums(g):
             nc.vector.bn_stats(out=stats[:, g, :], in_=x_sb[:, g, :])
+
+        def mean_and_variance(g):
             nc.vector.bn_aggr(out=mean_var[:, g, :], in_=stats[:, g, :])
 
-        def standard_deviation(groups):
+        def reciprocal_deviation(g):
             nc.scalar.activation(
-                out=std[:, groups], in_=mean_var[:, groups, 1], func=ACT.Sqrt, bias=eps_col[:], scale=1.0
+                out=rstd[:, g : g + 1],
+                in_=mean_var[:, g, 1:2],
+                func=ACT.Abs_reciprocal_sqrt,
+                bias=eps_col[:],
+                scale=1.0,
             )
-
-        def scale_and_shift_of_rows(groups):
-            nc.vector.reciprocal(out=rstd[:, groups], in_=std[:, groups])
-            nc.vector.tensor_scalar_mul(out=neg_mean[:, groups], in0=mean_var[:, groups, 0], scalar1=-1.0)
 
         def normalise(g):
             z = work.tile([P, PACK, P], F32)
-            nc.gpsimd.tensor_scalar(
+            nc.vector.tensor_scalar(
                 out=z[:],
                 in0=x_sb[:, g, :].rearrange("r (p t) -> r t p", t=PACK),
-                scalar1=neg_mean[:, g : g + 1],
+                scalar1=mean_var[:, g, 0:1],
                 scalar2=rstd[:, g : g + 1],
-                op0=ALU.add,
+                op0=ALU.subtract,
                 op1=ALU.mult,
             )
+            return z
+
+        def transpose(g, z):
             z_t = psum_t.tile([P, PACK, ROWS], F32, tag="transposed")
             for t in range(PACK):
                 nc.tensor.transpose(z_t[:, t, :], z[:, t, :], ident[:])
@@ -190,7 +196,7 @@ def tile_groupedlinear_e_kernel(tc, x, ln_gamma, ln_beta, W_words, W_scales, b, 
             y_ps_of[g] = y_ps
 
         def add_bias_and_store(g):
-            if g % VECTOR_SHARE == 0:
+            if g >= GROUPS - VECTOR_TAIL:
                 nc.vector.tensor_tensor(
                     out=y_sb[:, g, :, :],
                     in0=y_ps_of[g][:],
@@ -211,29 +217,34 @@ def tile_groupedlinear_e_kernel(tc, x, ln_gamma, ln_beta, W_words, W_scales, b, 
         def is_group(g):
             return 0 <= g < GROUPS
 
-        for tick in range(-STATS_AHEAD, GROUPS + 4 * STAGE_LAG):
+        for tick in range(-STATS_AHEAD, GROUPS + 4):
             g_stats = tick + STATS_AHEAD
-            g_scale = tick - STAGE_LAG
-            g_pack = tick - 2 * STAGE_LAG
-            g_multiply = tick - 3 * STAGE_LAG
-            g_store = tick - 4 * STAGE_LAG
+            g_scale = tick - 1
+            g_pack = tick - 2
+            g_multiply = tick - 3
+            g_store = tick - 4
+            if is_group(g_stats):
+                sums(g_stats)
             if is_group(g_pack):
                 regroup(g_pack)
             if is_group(g_stats):
                 mean_and_variance(g_stats)
+            z = normalise(tick) if is_group(tick) else None
             if is_group(g_pack):
                 quantise(g_pack)
-            if is_group(g_stats - 1) and g_stats % PAIR == 0:
-                scale_and_shift_of_rows(slice(g_stats - PAIR, g_stats))
+            if tick == -STATS_AHEAD:
+                widen_gamma_beta()
+            if is_group(g_stats - 1):
+                reciprocal_deviation(g_stats - 1)
+            if tick == -STATS_AHEAD + 1:
+                widen_bias()
+            if is_group(g_multiply):
+                multiply(g_multiply)
             if is_group(tick):
-                normalise(tick)
+                transpose(tick, z)
             if g_scale == 0:
                 keep_parameters()
             if is_group(g_scale):
                 scale_shift(g_scale)
-            if is_group(g_multiply):
-                multiply(g_multiply)
             if is_group(g_store):
                 add_bias_and_store(g_store)
-            if is_group(g_stats) and g_stats % PAIR == PAIR - 1:
-                standard_deviation(slice(g_stats + 1 - PAIR, g_stats + 1))

@@ -52,16 +52,17 @@ def tile_groupedlinear_e_kernel(tc, x, ln_gamma, ln_beta, W_words, W_scales, b, 
         xn_codes = keep.tile([P, GROUPS, ROWS], U32, align_bytes=64)
         xn_planes = keep.tile([P, GROUPS, ROWS], U8, align_bytes=64)
         y_sb = keep.tile([P, GROUPS, O_TILES, ROWS], F32)
-        par_rows = keep.tile([P, K], BF16)
+        gamma_beta_rows = keep.tile([P, K], BF16)
+        bias_rows = keep.tile([P, K], BF16)
         eps_col = keep.tile([P, 1], F32)
 
-        nc.vector.memset(par_rows[:], 0.0)
+        nc.scalar.dma_start(out=gamma_beta_rows[0:GROUPS, :], in_=ln_gamma)
+        nc.scalar.dma_start(out=gamma_beta_rows[GROUPS : 2 * GROUPS, :], in_=ln_beta)
         nc.vector.memset(eps_col[:], EPS)
+        nc.vector.memset(gamma_beta_rows[QUADRANT : 2 * QUADRANT, :], 0.0)
+        nc.vector.memset(gamma_beta_rows[2 * QUADRANT : P, :], 0.0)
+        nc.vector.memset(bias_rows[:], 0.0)
         nc.vector.memset(w_planes[:].bitcast(I32), 0)
-
-        nc.scalar.dma_start(out=par_rows[0:GROUPS, :], in_=ln_gamma)
-        nc.scalar.dma_start(out=par_rows[GROUPS : 2 * GROUPS, :], in_=ln_beta)
-        nc.scalar.dma_start(out=par_rows[2 * GROUPS : 3 * GROUPS, :], in_=b)
 
         def load_x(first, count):
             nc.sync.dma_start(out=x_sb[:, first : first + count, :], in_=x_rows[:, first : first + count, :])
@@ -78,6 +79,7 @@ def tile_groupedlinear_e_kernel(tc, x, ln_gamma, ln_beta, W_words, W_scales, b, 
         load_x(0, 1)
         load_x(1, 1)
         load_x(2, 2)
+        nc.sync.dma_start(out=bias_rows[0:GROUPS, :], in_=b)
         load_x(4, 4)
         load_weight(0)
         load_x(8, 4)
@@ -91,27 +93,24 @@ def tile_groupedlinear_e_kernel(tc, x, ln_gamma, ln_beta, W_words, W_scales, b, 
 
         ident = keep.tile([P, P], F32)
         make_identity(nc, ident[:])
+        ident_bf16 = keep.tile([P, P], BF16)
+        make_identity(nc, ident_bf16[:])
 
-        par_by_t = keep.tile([P, PACK, P], F32)
-        par_by_c = keep.tile([P, O_TILES, P], F32)
-        par_t_ps = psum_t.tile([P, PACK, P], F32, tag="transposed")
-        par_c_ps = psum_t.tile([P, O_TILES, P], F32, tag="transposed")
+        gamma_beta_ps = psum_t.tile([P, PACK, P], BF16, tag="transposed")
+        bias_ps = psum_t.tile([P, O_TILES, P], BF16, tag="transposed")
         gamma_beta = keep.tile([P, PACK, 2 * GROUPS], F32)
         bias_cols = keep.tile([P, O_TILES, GROUPS], F32)
 
-        def widen_gamma_beta():
-            nc.scalar.activation(out=par_by_t[:], in_=par_rows[:].rearrange("r (p t) -> r t p", t=PACK), func=ACT.Copy)
+        def turn_gamma_beta():
+            by_t = gamma_beta_rows[:].rearrange("r (p t) -> r t p", t=PACK)
             for t in range(PACK):
-                nc.tensor.transpose(par_t_ps[:, t, :], par_by_t[:, t, :], ident[:])
+                nc.tensor.transpose(gamma_beta_ps[:, t, :], by_t[:, t, :], ident_bf16[:])
+            nc.scalar.copy(out=gamma_beta[:], in_=gamma_beta_ps[:, :, 0 : 2 * GROUPS])
 
-        def widen_bias():
-            nc.scalar.activation(out=par_by_c[:], in_=par_rows[:].rearrange("r (c m) -> r c m", c=O_TILES), func=ACT.Copy)
+        def turn_bias():
             for c in range(O_TILES):
-                nc.tensor.transpose(par_c_ps[:, c, :], par_by_c[:, c, :], ident[:])
-
-        def keep_parameters():
-            nc.scalar.copy(out=gamma_beta[:], in_=par_t_ps[:, :, 0 : 2 * GROUPS])
-            nc.scalar.copy(out=bias_cols[:], in_=par_c_ps[:, :, 2 * GROUPS : 3 * GROUPS])
+                nc.tensor.transpose(bias_ps[:, c, :], bias_rows[:, c * P : (c + 1) * P], ident_bf16[:])
+            nc.scalar.copy(out=bias_cols[:], in_=bias_ps[:, :, 0:GROUPS])
 
         stats = keep.tile([P, GROUPS, BN_STATS_DIM], F32)
         mean_var = keep.tile([P, GROUPS, 2], F32)
@@ -233,18 +232,16 @@ def tile_groupedlinear_e_kernel(tc, x, ln_gamma, ln_beta, W_words, W_scales, b, 
             if is_group(g_pack):
                 quantise(g_pack)
             if tick == -STATS_AHEAD:
-                widen_gamma_beta()
+                turn_gamma_beta()
             if is_group(g_stats - 1):
                 reciprocal_deviation(g_stats - 1)
-            if tick == -STATS_AHEAD + 1:
-                widen_bias()
+            if tick == 0:
+                turn_bias()
             if is_group(g_multiply):
                 multiply(g_multiply)
-            if is_group(tick):
-                transpose(tick, z)
-            if g_scale == 0:
-                keep_parameters()
-            if is_group(g_scale):
-                scale_shift(g_scale)
             if is_group(g_store):
                 add_bias_and_store(g_store)
+            if is_group(tick):
+                transpose(tick, z)
+            if is_group(g_scale):
+                scale_shift(g_scale)

@@ -26,6 +26,7 @@ PLANES = 4
 
 STATS_AHEAD = 2
 VECTOR_TAIL = 2
+HEAD = 3
 LIVE = 4
 
 FLOPS = 2 * GROUPS * ROWS * K * N_OUT
@@ -115,6 +116,7 @@ def tile_groupedlinear_e_kernel(tc, x, ln_gamma, ln_beta, W_words, W_scales, b, 
         stats = keep.tile([P, GROUPS, BN_STATS_DIM], F32)
         mean_var = keep.tile([P, GROUPS, 2], F32)
         rstd = keep.tile([P, GROUPS], F32)
+        neg_mean = keep.tile([P, HEAD], F32)
         z_t_of = {}
         xn_by_t_of = {}
         xn_words_of = {}
@@ -134,17 +136,30 @@ def tile_groupedlinear_e_kernel(tc, x, ln_gamma, ln_beta, W_words, W_scales, b, 
                 bias=eps_col[:],
                 scale=1.0,
             )
+            if g < HEAD:
+                nc.scalar.activation(out=neg_mean[:, g : g + 1], in_=mean_var[:, g, 0:1], func=ACT.Copy, scale=-1.0)
 
         def normalise(g):
             z = work.tile([P, PACK, P], F32)
-            nc.vector.tensor_scalar(
-                out=z[:],
-                in0=x_sb[:, g, :].rearrange("r (p t) -> r t p", t=PACK),
-                scalar1=mean_var[:, g, 0:1],
-                scalar2=rstd[:, g : g + 1],
-                op0=ALU.subtract,
-                op1=ALU.mult,
-            )
+            by_t = x_sb[:, g, :].rearrange("r (p t) -> r t p", t=PACK)
+            if g < HEAD:
+                nc.gpsimd.tensor_scalar(
+                    out=z[:],
+                    in0=by_t,
+                    scalar1=neg_mean[:, g : g + 1],
+                    scalar2=rstd[:, g : g + 1],
+                    op0=ALU.add,
+                    op1=ALU.mult,
+                )
+            else:
+                nc.vector.tensor_scalar(
+                    out=z[:],
+                    in0=by_t,
+                    scalar1=mean_var[:, g, 0:1],
+                    scalar2=rstd[:, g : g + 1],
+                    op0=ALU.subtract,
+                    op1=ALU.mult,
+                )
             return z
 
         def transpose(g, z):
@@ -167,7 +182,10 @@ def tile_groupedlinear_e_kernel(tc, x, ln_gamma, ln_beta, W_words, W_scales, b, 
 
         def regroup(g):
             xn_words = work.tile([P, ROWS, PACK], BF16, align_bytes=64)
-            nc.vector.tensor_copy(out=xn_words[:], in_=xn_by_t_of[g][:].rearrange("p t r -> p r t"))
+            nc.vector.tensor_copy(
+                out=xn_words[:].rearrange("p (c i) t -> p c t i", i=4),
+                in_=xn_by_t_of[g][:].rearrange("p t (c i) -> p c t i", i=4),
+            )
             xn_words_of[g] = xn_words
 
         def quantise(g):

@@ -25,7 +25,6 @@ QUADRANT = 32
 PLANES = 4
 
 STATS_AHEAD = 2
-VECTOR_TAIL = 2
 HEAD = 3
 LIVE = 4
 
@@ -75,7 +74,10 @@ def tile_groupedlinear_e_kernel(tc, x, ln_gamma, ln_beta, W_words, W_scales, b, 
                     out=w_planes[quad * QUADRANT : quad * QUADRANT + 4 * PLANES, a, :].bitcast(I32),
                     in_=w_scales_hbm[groups, 4 * quad : 4 * quad + 4, :],
                 )
-            nc.sync.dma_start(out=w_sb[:, groups, :], in_=w_words_hbm[:, groups, :])
+            pieces = 2 if a == 0 else 1
+            step = PLANES // pieces
+            for first in range(a * PLANES, (a + 1) * PLANES, step):
+                nc.sync.dma_start(out=w_sb[:, first : first + step, :], in_=w_words_hbm[:, first : first + step, :])
 
         load_x(0, 1)
         load_x(1, 1)
@@ -198,11 +200,16 @@ def tile_groupedlinear_e_kernel(tc, x, ln_gamma, ln_beta, W_words, W_scales, b, 
         def multiply(g):
             a = g // PLANES
             first_row = 4 * (g % PLANES)
-            y_ps = psum_y.tile([P, O_TILES, ROWS], F32)
+            banks = 2 if g == GROUPS - 1 else 1
+            per_bank = O_TILES // banks
+            y_banks = []
+            for h in range(banks):
+                y_ps = psum_y.tile([P, per_bank, ROWS], F32)
+                y_banks.append(y_ps)
             for c in range(O_TILES):
                 cols = slice(c * P, (c + 1) * P)
                 nc.tensor.matmul_mx(
-                    out=y_ps[:, c, :],
+                    out=y_banks[c // per_bank][:, c % per_bank, :],
                     lhsT=w_sb[:, g, cols].bitcast(FP8X4),
                     lhsT_scale=w_planes[first_row:P, a, cols],
                     rhs=xn_codes[:, g, :].bitcast(FP8X4),
@@ -210,26 +217,30 @@ def tile_groupedlinear_e_kernel(tc, x, ln_gamma, ln_beta, W_words, W_scales, b, 
                     start=True,
                     stop=True,
                 )
-            y_ps_of[g] = y_ps
+            y_ps_of[g] = y_banks
 
         def add_bias_and_store(g):
-            if g >= GROUPS - VECTOR_TAIL:
-                nc.vector.tensor_tensor(
-                    out=y_sb[:, g, :, :],
-                    in0=y_ps_of[g][:],
-                    in1=bias_cols[:, :, g : g + 1].to_broadcast([P, O_TILES, ROWS]),
-                    op=ALU.add,
-                )
-            else:
-                for c in range(O_TILES):
-                    nc.scalar.activation(
-                        out=y_sb[:, g, c, :],
-                        in_=y_ps_of[g][:, c, :],
-                        func=ACT.Identity,
-                        bias=bias_cols[:, c, g : g + 1],
-                        scale=1.0,
+            y_banks = y_ps_of[g]
+            per_bank = O_TILES // len(y_banks)
+            for h in range(len(y_banks)):
+                tiles = slice(h * per_bank, (h + 1) * per_bank)
+                if g == GROUPS - 2 or (g == GROUPS - 1 and h == 0):
+                    nc.vector.tensor_tensor(
+                        out=y_sb[:, g, tiles, :],
+                        in0=y_banks[h][:],
+                        in1=bias_cols[:, tiles, g : g + 1].to_broadcast([P, per_bank, ROWS]),
+                        op=ALU.add,
                     )
-            nc.sync.dma_start(out=out_rows[:, g, :, :], in_=y_sb[:, g, :, :])
+                else:
+                    for c in range(per_bank):
+                        nc.scalar.activation(
+                            out=y_sb[:, g, h * per_bank + c, :],
+                            in_=y_banks[h][:, c, :],
+                            func=ACT.Identity,
+                            bias=bias_cols[:, h * per_bank + c, g : g + 1],
+                            scale=1.0,
+                        )
+                nc.sync.dma_start(out=out_rows[:, g, tiles, :], in_=y_sb[:, g, tiles, :])
 
         def is_group(g):
             return 0 <= g < GROUPS

@@ -245,12 +245,12 @@ def tile_groupedlinear_e_kernel(tc, x, ln_gamma, ln_beta, W_words, W_scales, b, 
         def is_group(g):
             return 0 <= g < GROUPS
 
-        for tick in range(-STATS_AHEAD, GROUPS + 4):
+        for tick in range(-STATS_AHEAD, GROUPS + 5):
             g_stats = tick + STATS_AHEAD
             g_scale = tick - 1
-            g_pack = tick - 2
-            g_multiply = tick - 3
-            g_store = tick - 4
+            g_pack = tick - 3
+            g_multiply = tick - 4
+            g_store = tick - 5
             if is_group(g_stats):
                 sums(g_stats)
             if is_group(g_pack):

@@ -26,6 +26,7 @@ PLANES = 4
 
 STATS_AHEAD = 2
 HEAD = 3
+SCALAR_STATS = 1
 LIVE = 4
 
 FLOPS = 2 * GROUPS * ROWS * K * N_OUT
@@ -141,6 +142,28 @@ def tile_groupedlinear_e_kernel(tc, x, ln_gamma, ln_beta, W_words, W_scales, b, 
             if g < HEAD:
                 nc.scalar.activation(out=neg_mean[:, g : g + 1], in_=mean_var[:, g, 0:1], func=ACT.Copy, scale=-1.0)
 
+        row_sum = keep.tile([P, 1], F32)
+        row_squares = keep.tile([P, 1], F32)
+
+        def scalar_sum(g):
+            unused = work.tile([P, K], BF16)
+            nc.scalar.activation(out=unused[:], in_=x_sb[:, g, :], func=ACT.Copy, accum_out=row_sum[:])
+
+        def scalar_deviation(g):
+            nc.scalar.activation(out=neg_mean[:, g : g + 1], in_=row_sum[:], func=ACT.Copy, scale=-1.0 / K)
+            unused = work.tile([P, K], BF16)
+            nc.scalar.activation(
+                out=unused[:],
+                in_=x_sb[:, g, :],
+                func=ACT.Square,
+                bias=neg_mean[:, g : g + 1],
+                scale=1.0,
+                accum_out=row_squares[:],
+            )
+            nc.scalar.activation(
+                out=rstd[:, g : g + 1], in_=row_squares[:], func=ACT.Abs_reciprocal_sqrt, bias=eps_col[:], scale=1.0 / K
+            )
+
         def normalise(g):
             z = work.tile([P, PACK, P], F32)
             by_t = x_sb[:, g, :].rearrange("r (p t) -> r t p", t=PACK)
@@ -251,19 +274,22 @@ def tile_groupedlinear_e_kernel(tc, x, ln_gamma, ln_beta, W_words, W_scales, b, 
             g_pack = tick - 3
             g_multiply = tick - 4
             g_store = tick - 5
-            if is_group(g_stats):
+            if is_group(g_stats) and g_stats != SCALAR_STATS:
                 sums(g_stats)
             if is_group(g_pack):
                 regroup(g_pack)
-            if is_group(g_stats):
-                mean_and_variance(g_stats)
             z = normalise(tick) if is_group(tick) else None
+            if is_group(g_stats) and g_stats != SCALAR_STATS:
+                mean_and_variance(g_stats)
             if is_group(g_pack):
                 quantise(g_pack)
             if tick == -STATS_AHEAD:
+                scalar_sum(SCALAR_STATS)
                 turn_gamma_beta()
-            if is_group(g_stats - 1):
+            if is_group(g_stats - 1) and g_stats - 1 != SCALAR_STATS:
                 reciprocal_deviation(g_stats - 1)
+            if g_stats == SCALAR_STATS:
+                scalar_deviation(SCALAR_STATS)
             if tick == 0:
                 turn_bias()
             if is_group(g_multiply):

@@ -27,6 +27,7 @@ PLANES = 4
 STATS_AHEAD = 2
 HEAD = 3
 SCALAR_STATS = 1
+GPSIMD_NORMALISES = (1, 2)
 LIVE = 4
 
 FLOPS = 2 * GROUPS * ROWS * K * N_OUT
@@ -60,10 +61,14 @@ def tile_groupedlinear_e_kernel(tc, x, ln_gamma, ln_beta, W_words, W_scales, b, 
         nc.scalar.dma_start(out=gamma_beta_rows[0:GROUPS, :], in_=ln_gamma)
         nc.scalar.dma_start(out=gamma_beta_rows[GROUPS : 2 * GROUPS, :], in_=ln_beta)
         nc.vector.memset(eps_col[:], EPS)
-        nc.vector.memset(gamma_beta_rows[QUADRANT : 2 * QUADRANT, :], 0.0)
-        nc.vector.memset(gamma_beta_rows[2 * QUADRANT : P, :], 0.0)
-        nc.vector.memset(bias_rows[:], 0.0)
-        nc.vector.memset(w_planes[:].bitcast(I32), 0)
+        nc.vector.memset(gamma_beta_rows[QUADRANT : 2 * QUADRANT, :].bitcast(I32), 0)
+        nc.vector.memset(gamma_beta_rows[2 * QUADRANT : P, :].bitcast(I32), 0)
+        nc.vector.memset(bias_rows[:].bitcast(I32), 0)
+        ident_bf16 = keep.tile([P, P], BF16)
+        make_identity(nc, ident_bf16[:])
+        nc.gpsimd.memset(w_planes[:].bitcast(I32), 0)
+        ident = keep.tile([P, P], F32)
+        make_identity(nc, ident[:])
 
         def load_x(first, count):
             nc.sync.dma_start(out=x_sb[:, first : first + count, :], in_=x_rows[:, first : first + count, :])
@@ -94,11 +99,6 @@ def tile_groupedlinear_e_kernel(tc, x, ln_gamma, ln_beta, W_words, W_scales, b, 
 
         first_rstd = keep.tile([P, 1], F32)
         nc.scalar.activation(out=first_rstd[:], in_=eps_col[:], func=ACT.Abs_reciprocal_sqrt)
-
-        ident = keep.tile([P, P], F32)
-        make_identity(nc, ident[:])
-        ident_bf16 = keep.tile([P, P], BF16)
-        make_identity(nc, ident_bf16[:])
 
         gamma_beta_ps = psum_t.tile([P, PACK, P], BF16, tag="transposed")
         bias_ps = psum_t.tile([P, O_TILES, P], BF16, tag="transposed")
@@ -139,7 +139,7 @@ def tile_groupedlinear_e_kernel(tc, x, ln_gamma, ln_beta, W_words, W_scales, b, 
                 bias=eps_col[:],
                 scale=1.0,
             )
-            if g < HEAD:
+            if g in GPSIMD_NORMALISES:
                 nc.scalar.activation(out=neg_mean[:, g : g + 1], in_=mean_var[:, g, 0:1], func=ACT.Copy, scale=-1.0)
 
         row_sum = keep.tile([P, 1], F32)
@@ -167,7 +167,7 @@ def tile_groupedlinear_e_kernel(tc, x, ln_gamma, ln_beta, W_words, W_scales, b, 
         def normalise(g):
             z = work.tile([P, PACK, P], F32)
             by_t = x_sb[:, g, :].rearrange("r (p t) -> r t p", t=PACK)
-            if g < HEAD:
+            if g in GPSIMD_NORMALISES:
                 nc.gpsimd.tensor_scalar(
                     out=z[:],
                     in0=by_t,
@@ -268,6 +268,18 @@ def tile_groupedlinear_e_kernel(tc, x, ln_gamma, ln_beta, W_words, W_scales, b, 
         def is_group(g):
             return 0 <= g < GROUPS
 
+        def aggregated_in(tick):
+            newest = tick + STATS_AHEAD
+            if newest == 0:
+                groups = [0]
+            elif tick < HEAD:
+                groups = [newest - 1]
+            elif tick == HEAD:
+                groups = [newest - 1, newest]
+            else:
+                groups = [newest]
+            return [g for g in groups if is_group(g) and g != SCALAR_STATS and not (g == 0 and newest == 1)]
+
         for tick in range(-STATS_AHEAD, GROUPS + 5):
             g_stats = tick + STATS_AHEAD
             g_scale = tick - 1
@@ -279,8 +291,8 @@ def tile_groupedlinear_e_kernel(tc, x, ln_gamma, ln_beta, W_words, W_scales, b, 
             if is_group(g_pack):
                 regroup(g_pack)
             z = normalise(tick) if is_group(tick) else None
-            if is_group(g_stats) and g_stats != SCALAR_STATS:
-                mean_and_variance(g_stats)
+            for g in aggregated_in(tick):
+                mean_and_variance(g)
             if is_group(g_pack):
                 quantise(g_pack)
             if tick == -STATS_AHEAD:

@@ -220,15 +220,21 @@ def tile_groupedlinear_e_kernel(tc, x, ln_gamma, ln_beta, W_words, W_scales, b, 
                 in_=xn_words_of[g][:].rearrange("p r t -> p (r t)"),
             )
 
+        def take_banks(g):
+            if g not in y_ps_of:
+                banks = 2 if g == GROUPS - 1 else 1
+                y_banks = []
+                for h in range(banks):
+                    y_ps = psum_y.tile([P, O_TILES // banks, ROWS], F32)
+                    y_banks.append(y_ps)
+                y_ps_of[g] = y_banks
+            return y_ps_of[g]
+
         def multiply(g):
             a = g // PLANES
             first_row = 4 * (g % PLANES)
-            banks = 2 if g == GROUPS - 1 else 1
-            per_bank = O_TILES // banks
-            y_banks = []
-            for h in range(banks):
-                y_ps = psum_y.tile([P, per_bank, ROWS], F32)
-                y_banks.append(y_ps)
+            y_banks = take_banks(g)
+            per_bank = O_TILES // len(y_banks)
             for c in range(O_TILES):
                 cols = slice(c * P, (c + 1) * P)
                 nc.tensor.matmul_mx(
@@ -240,7 +246,16 @@ def tile_groupedlinear_e_kernel(tc, x, ln_gamma, ln_beta, W_words, W_scales, b, 
                     start=True,
                     stop=True,
                 )
-            y_ps_of[g] = y_banks
+            if g + 1 < GROUPS - 1:
+                nc.tensor.matmul_mx(
+                    out=take_banks(g + 1)[0][:].rearrange("p c r -> p (c r)"),
+                    lhsT=xn_codes[:, g, :].bitcast(FP8X4),
+                    lhsT_scale=xn_planes[:, g, :],
+                    rhs=w_sb[:, g, :].bitcast(FP8X4),
+                    rhs_scale=w_planes[first_row:P, a, :],
+                    start=True,
+                    stop=True,
+                )
 
         def add_bias_and_store(g):
             y_banks = y_ps_of[g]

@@ -28,6 +28,7 @@ STATS_AHEAD = 2
 HEAD = 3
 SCALAR_STATS = 1
 GPSIMD_NORMALISES = (1, 2)
+WARM_UP_BLOCKS = 6
 LIVE = 4
 
 FLOPS = 2 * GROUPS * ROWS * K * N_OUT
@@ -230,6 +231,16 @@ def tile_groupedlinear_e_kernel(tc, x, ln_gamma, ln_beta, W_words, W_scales, b, 
                 y_ps_of[g] = y_banks
             return y_ps_of[g]
 
+        def warm_up(moving):
+            columns = moving.shape[-1]
+            nc.tensor.matmul(
+                take_banks(0)[0][:].rearrange("p c r -> p (c r)")[:, 0:columns],
+                ident_bf16[:],
+                moving,
+                start=True,
+                stop=True,
+            )
+
         def multiply(g):
             a = g // PLANES
             first_row = 4 * (g % PLANES)
@@ -312,6 +323,8 @@ def tile_groupedlinear_e_kernel(tc, x, ln_gamma, ln_beta, W_words, W_scales, b, 
                 quantise(g_pack)
             if tick == -STATS_AHEAD:
                 scalar_sum(SCALAR_STATS)
+                for i in range(WARM_UP_BLOCKS):
+                    warm_up(ident_bf16[:])
                 turn_gamma_beta()
             if is_group(g_stats - 1) and g_stats - 1 != SCALAR_STATS:
                 reciprocal_deviation(g_stats - 1)
@@ -323,7 +336,11 @@ def tile_groupedlinear_e_kernel(tc, x, ln_gamma, ln_beta, W_words, W_scales, b, 
                 multiply(g_multiply)
             if is_group(g_store):
                 add_bias_and_store(g_store)
+            if tick == 0:
+                warm_up(x_sb[:, 0, :])
             if is_group(tick):
                 transpose(tick, z)
+            if 0 <= tick < 3:
+                warm_up(x_sb[:, 0, :])
             if is_group(g_scale):
                 scale_shift(g_scale)

@@ -29,6 +29,8 @@ HEAD = 3
 SCALAR_STATS = 1
 GPSIMD_NORMALISES = (1, 2)
 WARM_UP_BLOCKS = 6
+SCALAR_REGROUPS = (4,)
+VECTOR_BIAS = (10, 14)
 LIVE = 4
 
 FLOPS = 2 * GROUPS * ROWS * K * N_OUT
@@ -45,7 +47,8 @@ def tile_groupedlinear_e_kernel(tc, x, ln_gamma, ln_beta, W_words, W_scales, b, 
     with ExitStack() as ctx:
         keep = ctx.enter_context(tc.tile_pool(name="keep", bufs=1))
         work = ctx.enter_context(tc.tile_pool(name="work", bufs=LIVE))
-        psum_t = ctx.enter_context(tc.psum_pool(name="psum_t", bufs=LIVE))
+        psum_t = ctx.enter_context(tc.psum_pool(name="psum_t", bufs=LIVE - 1))
+        psum_unread = ctx.enter_context(tc.psum_pool(name="psum_unread", bufs=1))
         psum_y = ctx.enter_context(tc.psum_pool(name="psum_y", bufs=LIVE))
         ctx.enter_context(tc.manual_schedule())
 
@@ -74,33 +77,35 @@ def tile_groupedlinear_e_kernel(tc, x, ln_gamma, ln_beta, W_words, W_scales, b, 
         def load_x(first, count):
             nc.sync.dma_start(out=x_sb[:, first : first + count, :], in_=x_rows[:, first : first + count, :])
 
-        def load_weight(a):
+        def load_scales(a):
             groups = slice(a * PLANES, (a + 1) * PLANES)
             for quad in range(P // QUADRANT):
                 nc.sync.dma_start(
                     out=w_planes[quad * QUADRANT : quad * QUADRANT + 4 * PLANES, a, :].bitcast(I32),
                     in_=w_scales_hbm[groups, 4 * quad : 4 * quad + 4, :],
                 )
-            pieces = 2 if a == 0 else 1
-            step = PLANES // pieces
-            for first in range(a * PLANES, (a + 1) * PLANES, step):
-                nc.sync.dma_start(out=w_sb[:, first : first + step, :], in_=w_words_hbm[:, first : first + step, :])
+
+        def load_words(first, count):
+            nc.sync.dma_start(out=w_sb[:, first : first + count, :], in_=w_words_hbm[:, first : first + count, :])
 
         load_x(0, 1)
         load_x(1, 1)
         load_x(2, 2)
         nc.sync.dma_start(out=bias_rows[0:GROUPS, :], in_=b)
         load_x(4, 4)
-        load_weight(0)
+        load_scales(0)
+        load_words(0, 2)
         load_x(8, 4)
+        load_words(2, 2)
         load_x(12, 4)
-        load_weight(1)
-        load_weight(2)
-        load_weight(3)
+        for a in range(1, GROUPS // PLANES):
+            load_scales(a)
+            load_words(a * PLANES, PLANES)
 
         first_rstd = keep.tile([P, 1], F32)
         nc.scalar.activation(out=first_rstd[:], in_=eps_col[:], func=ACT.Abs_reciprocal_sqrt)
 
+        unread = psum_unread.tile([P, N_OUT], F32)
         gamma_beta_ps = psum_t.tile([P, PACK, P], BF16, tag="transposed")
         bias_ps = psum_t.tile([P, O_TILES, P], BF16, tag="transposed")
         gamma_beta = keep.tile([P, PACK, 2 * GROUPS], F32)
@@ -208,7 +213,8 @@ def tile_groupedlinear_e_kernel(tc, x, ln_gamma, ln_beta, W_words, W_scales, b, 
 
         def regroup(g):
             xn_words = work.tile([P, ROWS, PACK], BF16, align_bytes=64)
-            nc.vector.tensor_copy(
+            copy = nc.scalar.copy if g in SCALAR_REGROUPS else nc.vector.tensor_copy
+            copy(
                 out=xn_words[:].rearrange("p (c i) t -> p c t i", i=4),
                 in_=xn_by_t_of[g][:].rearrange("p t (c i) -> p c t i", i=4),
             )
@@ -221,20 +227,10 @@ def tile_groupedlinear_e_kernel(tc, x, ln_gamma, ln_beta, W_words, W_scales, b, 
                 in_=xn_words_of[g][:].rearrange("p r t -> p (r t)"),
             )
 
-        def take_banks(g):
-            if g not in y_ps_of:
-                banks = 2 if g == GROUPS - 1 else 1
-                y_banks = []
-                for h in range(banks):
-                    y_ps = psum_y.tile([P, O_TILES // banks, ROWS], F32)
-                    y_banks.append(y_ps)
-                y_ps_of[g] = y_banks
-            return y_ps_of[g]
-
         def warm_up(moving):
             columns = moving.shape[-1]
             nc.tensor.matmul(
-                take_banks(0)[0][:].rearrange("p c r -> p (c r)")[:, 0:columns],
+                unread[:, 0:columns],
                 ident_bf16[:],
                 moving,
                 start=True,
@@ -244,8 +240,13 @@ def tile_groupedlinear_e_kernel(tc, x, ln_gamma, ln_beta, W_words, W_scales, b, 
         def multiply(g):
             a = g // PLANES
             first_row = 4 * (g % PLANES)
-            y_banks = take_banks(g)
-            per_bank = O_TILES // len(y_banks)
+            banks = 2 if g == GROUPS - 1 else 1
+            per_bank = O_TILES // banks
+            y_banks = []
+            for h in range(banks):
+                y_ps = psum_y.tile([P, per_bank, ROWS], F32)
+                y_banks.append(y_ps)
+            y_ps_of[g] = y_banks
             for c in range(O_TILES):
                 cols = slice(c * P, (c + 1) * P)
                 nc.tensor.matmul_mx(
@@ -257,9 +258,9 @@ def tile_groupedlinear_e_kernel(tc, x, ln_gamma, ln_beta, W_words, W_scales, b, 
                     start=True,
                     stop=True,
                 )
-            if g + 1 < GROUPS - 1:
+            if g < 10:
                 nc.tensor.matmul_mx(
-                    out=take_banks(g + 1)[0][:].rearrange("p c r -> p (c r)"),
+                    out=unread[:],
                     lhsT=xn_codes[:, g, :].bitcast(FP8X4),
                     lhsT_scale=xn_planes[:, g, :],
                     rhs=w_sb[:, g, :].bitcast(FP8X4),
@@ -273,7 +274,7 @@ def tile_groupedlinear_e_kernel(tc, x, ln_gamma, ln_beta, W_words, W_scales, b, 
             per_bank = O_TILES // len(y_banks)
             for h in range(len(y_banks)):
                 tiles = slice(h * per_bank, (h + 1) * per_bank)
-                if g == GROUPS - 2 or (g == GROUPS - 1 and h == 0):
+                if g in VECTOR_BIAS or (g == GROUPS - 1 and h == 0):
                     nc.vector.tensor_tensor(
                         out=y_sb[:, g, tiles, :],
                         in0=y_banks[h][:],
@@ -321,6 +322,8 @@ def tile_groupedlinear_e_kernel(tc, x, ln_gamma, ln_beta, W_words, W_scales, b, 
                 mean_and_variance(g)
             if is_group(g_pack):
                 quantise(g_pack)
+            if g_store in VECTOR_BIAS:
+                add_bias_and_store(g_store)
             if tick == -STATS_AHEAD:
                 scalar_sum(SCALAR_STATS)
                 for i in range(WARM_UP_BLOCKS):
@@ -334,7 +337,7 @@ def tile_groupedlinear_e_kernel(tc, x, ln_gamma, ln_beta, W_words, W_scales, b, 
                 turn_bias()
             if is_group(g_multiply):
                 multiply(g_multiply)
-            if is_group(g_store):
+            if is_group(g_store) and g_store not in VECTOR_BIAS:
                 add_bias_and_store(g_store)
             if tick == 0:
                 warm_up(x_sb[:, 0, :])

@@ -97,8 +97,11 @@ def tile_groupedlinear_e_kernel(tc, x, ln_gamma, ln_beta, W_words, W_scales, b, 
         load_words(0, 2)
         load_x(8, 4)
         load_words(2, 2)
+        load_scales(1)
+        load_words(4, 2)
+        load_words(6, 2)
         load_x(12, 4)
-        for a in range(1, GROUPS // PLANES):
+        for a in range(2, GROUPS // PLANES):
             load_scales(a)
             load_words(a * PLANES, PLANES)
 

from contextlib import ExitStack

import concourse.mybir as mybir
from concourse.masks import make_identity

F32 = mybir.dt.float32
BF16 = mybir.dt.bfloat16
I32 = mybir.dt.int32
U32 = mybir.dt.uint32
U8 = mybir.dt.uint8
FP8X4 = mybir.dt.float8_e4m3fn_x4
ACT = mybir.ActivationFunctionType
ALU = mybir.AluOpType

P = 128
PACK = 4
GROUPS = 16
ROWS = 128
K = 512
N_OUT = 512
O_TILES = N_OUT // P
EPS = 1e-6
BN_STATS_DIM = 6
QUADRANT = 32
PLANES = 4

STATS_AHEAD = 2
HEAD = 3
SCALAR_STATS = 1
GPSIMD_NORMALISES = (1, 2)
WARM_UP_BLOCKS = 6
SCALAR_REGROUPS = (4,)
VECTOR_BIAS = (10, 14)
LIVE = 4

FLOPS = 2 * GROUPS * ROWS * K * N_OUT


def tile_groupedlinear_e_kernel(tc, x, ln_gamma, ln_beta, W_words, W_scales, b, out):
    nc = tc.nc

    x_rows = x.rearrange("(g r c) h i j -> r g (c h i j)", g=GROUPS, r=ROWS)
    w_words_hbm = W_words.rearrange("g p n t -> p g (n t)").bitcast(I32)
    w_scales_hbm = W_scales.bitcast(I32)
    out_rows = out.rearrange("(g c m) h i j -> m g c (h i j)", g=GROUPS, c=O_TILES)

    with ExitStack() as ctx:
        keep = ctx.enter_context(tc.tile_pool(name="keep", bufs=1))
        work = ctx.enter_context(tc.tile_pool(name="work", bufs=LIVE))
        psum_t = ctx.enter_context(tc.psum_pool(name="psum_t", bufs=LIVE - 1))
        psum_unread = ctx.enter_context(tc.psum_pool(name="psum_unread", bufs=1))
        psum_y = ctx.enter_context(tc.psum_pool(name="psum_y", bufs=LIVE))
        ctx.enter_context(tc.manual_schedule())

        x_sb = keep.tile([P, GROUPS, K], BF16)
        w_sb = keep.tile([P, GROUPS, N_OUT], I32, align_bytes=64)
        w_planes = keep.tile([P, GROUPS // PLANES, N_OUT], U8, align_bytes=64)
        xn_codes = keep.tile([P, GROUPS, ROWS], U32, align_bytes=64)
        xn_planes = keep.tile([P, GROUPS, ROWS], U8, align_bytes=64)
        y_sb = keep.tile([P, GROUPS, O_TILES, ROWS], F32)
        gamma_beta_rows = keep.tile([P, K], BF16)
        bias_rows = keep.tile([P, K], BF16)
        eps_col = keep.tile([P, 1], F32)

        nc.scalar.dma_start(out=gamma_beta_rows[0:GROUPS, :], in_=ln_gamma)
        nc.scalar.dma_start(out=gamma_beta_rows[GROUPS : 2 * GROUPS, :], in_=ln_beta)
        nc.vector.memset(eps_col[:], EPS)
        nc.vector.memset(gamma_beta_rows[QUADRANT : 2 * QUADRANT, :].bitcast(I32), 0)
        nc.vector.memset(gamma_beta_rows[2 * QUADRANT : P, :].bitcast(I32), 0)
        nc.vector.memset(bias_rows[:].bitcast(I32), 0)
        ident_bf16 = keep.tile([P, P], BF16)
        make_identity(nc, ident_bf16[:])
        nc.gpsimd.memset(w_planes[:].bitcast(I32), 0)
        ident = keep.tile([P, P], F32)
        make_identity(nc, ident[:])

        def load_x(first, count):
            nc.sync.dma_start(out=x_sb[:, first : first + count, :], in_=x_rows[:, first : first + count, :])

        def load_scales(a):
            groups = slice(a * PLANES, (a + 1) * PLANES)
            for quad in range(P // QUADRANT):
                nc.sync.dma_start(
                    out=w_planes[quad * QUADRANT : quad * QUADRANT + 4 * PLANES, a, :].bitcast(I32),
                    in_=w_scales_hbm[groups, 4 * quad : 4 * quad + 4, :],
                )

        def load_words(first, count):
            nc.sync.dma_start(out=w_sb[:, first : first + count, :], in_=w_words_hbm[:, first : first + count, :])

        load_x(0, 1)
        load_x(1, 1)
        load_x(2, 2)
        nc.sync.dma_start(out=bias_rows[0:GROUPS, :], in_=b)
        load_x(4, 4)
        load_scales(0)
        load_words(0, 2)
        load_x(8, 4)
        load_words(2, 2)
        load_scales(1)
        load_words(4, 2)
        load_words(6, 2)
        load_x(12, 4)
        for a in range(2, GROUPS // PLANES):
            load_scales(a)
            load_words(a * PLANES, PLANES)

        first_rstd = keep.tile([P, 1], F32)
        nc.scalar.activation(out=first_rstd[:], in_=eps_col[:], func=ACT.Abs_reciprocal_sqrt)

        unread = psum_unread.tile([P, N_OUT], F32)
        gamma_beta_ps = psum_t.tile([P, PACK, P], BF16, tag="transposed")
        bias_ps = psum_t.tile([P, O_TILES, P], BF16, tag="transposed")
        gamma_beta = keep.tile([P, PACK, 2 * GROUPS], F32)
        bias_cols = keep.tile([P, O_TILES, GROUPS], F32)

        def turn_gamma_beta():
            by_t = gamma_beta_rows[:].rearrange("r (p t) -> r t p", t=PACK)
            for t in range(PACK):
                nc.tensor.transpose(gamma_beta_ps[:, t, :], by_t[:, t, :], ident_bf16[:])
            nc.scalar.copy(out=gamma_beta[:], in_=gamma_beta_ps[:, :, 0 : 2 * GROUPS])

        def turn_bias():
            for c in range(O_TILES):
                nc.tensor.transpose(bias_ps[:, c, :], bias_rows[:, c * P : (c + 1) * P], ident_bf16[:])
            nc.scalar.copy(out=bias_cols[:], in_=bias_ps[:, :, 0:GROUPS])

        stats = keep.tile([P, GROUPS, BN_STATS_DIM], F32)
        mean_var = keep.tile([P, GROUPS, 2], F32)
        rstd = keep.tile([P, GROUPS], F32)
        neg_mean = keep.tile([P, HEAD], F32)
        z_t_of = {}
        xn_by_t_of = {}
        xn_words_of = {}
        y_ps_of = {}

        def sums(g):
            nc.vector.bn_stats(out=stats[:, g, :], in_=x_sb[:, g, :])

        def mean_and_variance(g):
            nc.vector.bn_aggr(out=mean_var[:, g, :], in_=stats[:, g, :])

        def reciprocal_deviation(g):
            nc.scalar.activation(
                out=rstd[:, g : g + 1],
                in_=mean_var[:, g, 1:2],
                func=ACT.Abs_reciprocal_sqrt,
                bias=eps_col[:],
                scale=1.0,
            )
            if g in GPSIMD_NORMALISES:
                nc.scalar.activation(out=neg_mean[:, g : g + 1], in_=mean_var[:, g, 0:1], func=ACT.Copy, scale=-1.0)

        row_sum = keep.tile([P, 1], F32)
        row_squares = keep.tile([P, 1], F32)

        def scalar_sum(g):
            unused = work.tile([P, K], BF16)
            nc.scalar.activation(out=unused[:], in_=x_sb[:, g, :], func=ACT.Copy, accum_out=row_sum[:])

        def scalar_deviation(g):
            nc.scalar.activation(out=neg_mean[:, g : g + 1], in_=row_sum[:], func=ACT.Copy, scale=-1.0 / K)
            unused = work.tile([P, K], BF16)
            nc.scalar.activation(
                out=unused[:],
                in_=x_sb[:, g, :],
                func=ACT.Square,
                bias=neg_mean[:, g : g + 1],
                scale=1.0,
                accum_out=row_squares[:],
            )
            nc.scalar.activation(
                out=rstd[:, g : g + 1], in_=row_squares[:], func=ACT.Abs_reciprocal_sqrt, bias=eps_col[:], scale=1.0 / K
            )

        def normalise(g):
            z = work.tile([P, PACK, P], F32)
            by_t = x_sb[:, g, :].rearrange("r (p t) -> r t p", t=PACK)
            if g in GPSIMD_NORMALISES:
                nc.gpsimd.tensor_scalar(
                    out=z[:],
                    in0=by_t,
                    scalar1=neg_mean[:, g : g + 1],
                    scalar2=rstd[:, g : g + 1],
                    op0=ALU.add,
                    op1=ALU.mult,
                )
            else:
                nc.vector.tensor_scalar(
                    out=z[:],
                    in0=by_t,
                    scalar1=mean_var[:, g, 0:1],
                    scalar2=rstd[:, g : g + 1],
                    op0=ALU.subtract,
                    op1=ALU.mult,
                )
            return z

        def transpose(g, z):
            z_t = psum_t.tile([P, PACK, ROWS], F32, tag="transposed")
            for t in range(PACK):
                nc.tensor.transpose(z_t[:, t, :], z[:, t, :], ident[:])
            z_t_of[g] = z_t

        def scale_shift(g):
            xn_by_t = work.tile([P, PACK, ROWS], BF16)
            for t in range(PACK):
                nc.scalar.activation(
                    out=xn_by_t[:, t, :],
                    in_=z_t_of[g][:, t, :],
                    func=ACT.Identity,
                    scale=gamma_beta[:, t, g : g + 1],
                    bias=gamma_beta[:, t, GROUPS + g : GROUPS + g + 1],
                )
            xn_by_t_of[g] = xn_by_t

        def regroup(g):
            xn_words = work.tile([P, ROWS, PACK], BF16, align_bytes=64)
            copy = nc.scalar.copy if g in SCALAR_REGROUPS else nc.vector.tensor_copy
            copy(
                out=xn_words[:].rearrange("p (c i) t -> p c t i", i=4),
                in_=xn_by_t_of[g][:].rearrange("p t (c i) -> p c t i", i=4),
            )
            xn_words_of[g] = xn_words

        def quantise(g):
            nc.vector.quantize_mx(
                out=xn_codes[:, g, :].bitcast(FP8X4),
                scales=xn_planes[:, g, :],
                in_=xn_words_of[g][:].rearrange("p r t -> p (r t)"),
            )

        def warm_up(moving):
            columns = moving.shape[-1]
            nc.tensor.matmul(
                unread[:, 0:columns],
                ident_bf16[:],
                moving,
                start=True,
                stop=True,
            )

        def multiply(g):
            a = g // PLANES
            first_row = 4 * (g % PLANES)
            banks = 2 if g == GROUPS - 1 else 1
            per_bank = O_TILES // banks
            y_banks = []
            for h in range(banks):
                y_ps = psum_y.tile([P, per_bank, ROWS], F32)
                y_banks.append(y_ps)
            y_ps_of[g] = y_banks
            for c in range(O_TILES):
                cols = slice(c * P, (c + 1) * P)
                nc.tensor.matmul_mx(
                    out=y_banks[c // per_bank][:, c % per_bank, :],
                    lhsT=w_sb[:, g, cols].bitcast(FP8X4),
                    lhsT_scale=w_planes[first_row:P, a, cols],
                    rhs=xn_codes[:, g, :].bitcast(FP8X4),
                    rhs_scale=xn_planes[:, g, :],
                    start=True,
                    stop=True,
                )
            if g < 10:
                nc.tensor.matmul_mx(
                    out=unread[:],
                    lhsT=xn_codes[:, g, :].bitcast(FP8X4),
                    lhsT_scale=xn_planes[:, g, :],
                    rhs=w_sb[:, g, :].bitcast(FP8X4),
                    rhs_scale=w_planes[first_row:P, a, :],
                    start=True,
                    stop=True,
                )

        def add_bias_and_store(g):
            y_banks = y_ps_of[g]
            per_bank = O_TILES // len(y_banks)
            for h in range(len(y_banks)):
                tiles = slice(h * per_bank, (h + 1) * per_bank)
                if g in VECTOR_BIAS or (g == GROUPS - 1 and h == 0):
                    nc.vector.tensor_tensor(
                        out=y_sb[:, g, tiles, :],
                        in0=y_banks[h][:],
                        in1=bias_cols[:, tiles, g : g + 1].to_broadcast([P, per_bank, ROWS]),
                        op=ALU.add,
                    )
                else:
                    for c in range(per_bank):
                        nc.scalar.activation(
                            out=y_sb[:, g, h * per_bank + c, :],
                            in_=y_banks[h][:, c, :],
                            func=ACT.Identity,
                            bias=bias_cols[:, h * per_bank + c, g : g + 1],
                            scale=1.0,
                        )
                nc.sync.dma_start(out=out_rows[:, g, tiles, :], in_=y_sb[:, g, tiles, :])

        def is_group(g):
            return 0 <= g < GROUPS

        def aggregated_in(tick):
            newest = tick + STATS_AHEAD
            if newest == 0:
                groups = [0]
            elif tick < HEAD:
                groups = [newest - 1]
            elif tick == HEAD:
                groups = [newest - 1, newest]
            else:
                groups = [newest]
            return [g for g in groups if is_group(g) and g != SCALAR_STATS and not (g == 0 and newest == 1)]

        for tick in range(-STATS_AHEAD, GROUPS + 5):
            g_stats = tick + STATS_AHEAD
            g_scale = tick - 1
            g_pack = tick - 3
            g_multiply = tick - 4
            g_store = tick - 5
            if is_group(g_stats) and g_stats != SCALAR_STATS:
                sums(g_stats)
            if is_group(g_pack):
                regroup(g_pack)
            z = normalise(tick) if is_group(tick) else None
            for g in aggregated_in(tick):
                mean_and_variance(g)
            if is_group(g_pack):
                quantise(g_pack)
            if g_store in VECTOR_BIAS:
                add_bias_and_store(g_store)
            if tick == -STATS_AHEAD:
                scalar_sum(SCALAR_STATS)
                for i in range(WARM_UP_BLOCKS):
                    warm_up(ident_bf16[:])
                turn_gamma_beta()
            if is_group(g_stats - 1) and g_stats - 1 != SCALAR_STATS:
                reciprocal_deviation(g_stats - 1)
            if g_stats == SCALAR_STATS:
                scalar_deviation(SCALAR_STATS)
            if tick == 0:
                turn_bias()
            if is_group(g_multiply):
                multiply(g_multiply)
            if is_group(g_store) and g_store not in VECTOR_BIAS:
                add_bias_and_store(g_store)
            if tick == 0:
                warm_up(x_sb[:, 0, :])
            if is_group(tick):
                transpose(tick, z)
            if 0 <= tick < 3:
                warm_up(x_sb[:, 0, :])
            if is_group(g_scale):
                scale_shift(g_scale)
